import numpy as np
import ml_dtypes


def mxq(x, axis, fmt="e4m3"):
    dtype, down = {"e4m3": (ml_dtypes.float8_e4m3fn, 7), "e5m2": (ml_dtypes.float8_e5m2, 14)}[fmt]
    v = np.moveaxis(np.asarray(x, np.float32).astype(ml_dtypes.bfloat16).astype(np.float64), axis, -1)
    blocks = v.reshape(v.shape[:-1] + (-1, 32))
    amax = np.abs(blocks).max(-1, keepdims=True)
    byte = np.maximum(np.where(amax > 0, np.frexp(amax)[1] - 1 + 127, 0) - down, 1)
    scale = np.exp2(byte - 127.0)
    codes = (blocks / scale).astype(np.float32).astype(dtype).astype(np.float64)
    return np.moveaxis((codes * scale).reshape(v.shape), -1, axis)


WIDE = False


def mx_kscale(k):
    if not WIDE:
        return np.ones(k)
    levels = np.array([20, -20, 10, -10, 0])
    a = np.random.permutation(np.resize(levels, k // 512 * 4)).reshape(k // 512, 4)
    idx = np.arange(k)
    return np.exp2(a[idx // 512, idx % 128 // 32])


BF16 = ml_dtypes.bfloat16


def bf(x):
    return np.asarray(x, np.float32).astype(BF16)


def f64(x):
    return np.asarray(x).astype(np.float64)


N, C, F, H, W, KH, KW = 64, 64, 8192, 4, 4, 3, 3
P = H * W


def setup_inputs():
    u = mx_kscale(F)
    x = np.random.standard_normal((N, C, H, W)) * 2.0
    k = np.random.standard_normal((F, C, H, W)) * 2.0 / np.sqrt(C) / u[:, None, None, None]
    g = (np.random.standard_normal((N, F, H, W)) * np.exp2(np.random.randint(-12, 1, (N, 1, H, W)))
         * 4.0 * u[None, :, None, None])
    return {"x_dct": bf(x), "k_dct": bf(k), "grad_out": bf(g)}


def reference(x_dct, k_dct, grad_out):
    gq = mxq(f64(grad_out), 1, "e5m2").reshape(N, F, P).transpose(2, 0, 1)
    kq = mxq(f64(k_dct), 0, "e4m3").reshape(F, C, P).transpose(2, 0, 1)
    r = gq @ kq
    return r.transpose(1, 2, 0).reshape(N, C, H, W)

@@ -1,0 +1,135 @@
+import concourse.mybir as mybir
+
+BF16 = mybir.dt.bfloat16
+F32 = mybir.dt.float32
+U32 = mybir.dt.uint32
+U8 = mybir.dt.uint8
+E4M3X4 = mybir.dt.float8_e4m3fn_x4
+E5M2X4 = mybir.dt.float8_e5m2_x4
+
+P = 128
+IMAGES = 64
+CHANNELS = 64
+FILTERS = 8192
+FREQS = 16
+
+CLASSES = 4
+HALVES = 2
+PASSES_PER_CLASS = 4
+PACK = 4
+RUN = PASSES_PER_CLASS * PACK
+
+SLICES = 8
+IMAGE_CHUNK = 32
+CHUNKS = IMAGES // IMAGE_CHUNK
+N_MOVING = 512
+M_STATIONARY = 128
+
+FLOPS = 2 * FREQS * IMAGES * CHANNELS * FILTERS
+BYTES = 2 * FILTERS * FREQS * (IMAGES + CHANNELS) + 4 * IMAGES * CHANNELS * FREQS
+
+
+def tile_convdct_pa_k_kernel(tc, x_dct, k_dct, grad_out, out):
+    nc = tc.nc
+
+    g_dram = grad_out.rearrange(
+        "n (m cl hf e) y x -> cl hf m n (e y x)", m=64, cl=CLASSES, hf=HALVES, e=RUN
+    )
+    k_dram = k_dct.rearrange(
+        "(m cl hf e) c y x -> cl hf m e (c y x)", m=64, cl=CLASSES, hf=HALVES, e=RUN
+    )
+    out_dram = out.rearrange("n c (ph yl) x -> ph c n (yl x)", ph=2)
+
+    with tc.tile_pool(name="g_raw", bufs=3) as g_raw_pool, tc.tile_pool(
+        name="k_raw", bufs=4
+    ) as k_raw_pool, tc.tile_pool(name="g_grp", bufs=2) as g_grp_pool, tc.tile_pool(
+        name="k_grp", bufs=2
+    ) as k_grp_pool, tc.tile_pool(name="g_mx", bufs=2) as g_mx_pool, tc.tile_pool(
+        name="k_mx", bufs=3
+    ) as k_mx_pool, tc.tile_pool(name="result", bufs=1) as result_pool, tc.psum_pool(
+        name="acc", bufs=1
+    ) as acc_pool:
+        acc = [acc_pool.tile([P, N_MOVING], F32, name="acc%d" % sl) for sl in range(SLICES)]
+
+        for cl in range(CLASSES):
+            g_codes = g_mx_pool.tile([P, PASSES_PER_CLASS, 2, N_MOVING], U32, align_bytes=64)
+            g_scales = g_mx_pool.tile([P, PASSES_PER_CLASS, 2, N_MOVING], U8, align_bytes=64)
+            for chunk in range(CHUNKS):
+                images = slice(chunk * IMAGE_CHUNK, (chunk + 1) * IMAGE_CHUNK)
+                g_raw = g_raw_pool.tile([P, IMAGE_CHUNK, RUN * FREQS], BF16)
+                for hf in range(HALVES):
+                    nc.sync.dma_start(out=g_raw[hf:P:2, :, :], in_=g_dram[cl, hf, :, images, :])
+                g_rows = g_raw[:].rearrange(
+                    "q n (i j ph mg p2) -> q i mg n ph j p2", i=PASSES_PER_CLASS, j=PACK, ph=2, mg=2, p2=4
+                )
+                g_grp = g_grp_pool.tile([P, PASSES_PER_CLASS, 2, IMAGE_CHUNK * 8 * PACK], BF16, align_bytes=64)
+                for i in range(PASSES_PER_CLASS):
+                    for mg in range(2):
+                        g_words = g_grp[:, i, mg, :].rearrange(
+                            "q (n ph p2 j) -> q n ph j p2", n=IMAGE_CHUNK, ph=2, p2=4, j=PACK
+                        )
+                        if mg == 0:
+                            nc.vector.tensor_copy(out=g_words, in_=g_rows[:, i, mg])
+                        else:
+                            for ph in range(2):
+                                nc.scalar.copy(out=g_words[:, :, ph], in_=g_rows[:, i, mg, :, ph])
+                columns = slice(chunk * IMAGE_CHUNK * 8, (chunk + 1) * IMAGE_CHUNK * 8)
+                for i in range(PASSES_PER_CLASS):
+                    for mg in range(2):
+                        nc.vector.quantize_mx(
+                            out=g_codes[:, i, mg, columns].bitcast(E5M2X4),
+                            scales=g_scales[:, i, mg, columns],
+                            in_=g_grp[:, i, mg, :],
+                        )
+
+            for i in range(PASSES_PER_CLASS):
+                k_raw = k_raw_pool.tile([P, PACK, CHANNELS * FREQS], BF16)
+                for hf in range(HALVES):
+                    nc.sync.dma_start(
+                        out=k_raw[hf:P:2, :, :], in_=k_dram[cl, hf, :, i * PACK : (i + 1) * PACK, :]
+                    )
+                k_rows = k_raw[:].rearrange(
+                    "q j (c ph sc si) -> q ph sc c si j", c=CHANNELS, ph=2, sc=2, si=4
+                )
+                k_grp = k_grp_pool.tile([P, SLICES * M_STATIONARY * PACK], BF16, align_bytes=64)
+                k_words = k_grp[:].rearrange(
+                    "q (sc si ph c j) -> q ph sc c si j", sc=2, si=4, ph=2, c=CHANNELS, j=PACK
+                )
+                nc.vector.tensor_copy(out=k_words[:, 0], in_=k_rows[:, 0])
+                for sc in range(2):
+                    nc.scalar.copy(out=k_words[:, 1, sc], in_=k_rows[:, 1, sc])
+                k_codes = k_mx_pool.tile([P, SLICES * M_STATIONARY], U32, align_bytes=64)
+                k_scales = k_mx_pool.tile([P, SLICES * M_STATIONARY], U8, align_bytes=64)
+                nc.vector.quantize_mx(out=k_codes[:].bitcast(E4M3X4), scales=k_scales[:], in_=k_grp[:])
+
+                first = cl == 0 and i == 0
+                last = cl == CLASSES - 1 and i == PASSES_PER_CLASS - 1
+                for sl in range(SLICES):
+                    m_cols = slice(sl * M_STATIONARY, (sl + 1) * M_STATIONARY)
+                    nc.tensor.matmul_mx(
+                        out=acc[sl][:],
+                        lhsT=k_codes[:, m_cols].bitcast(E4M3X4),
+                        lhsT_scale=k_scales[:, m_cols],
+                        rhs=g_codes[:, i, sl // 4, :].bitcast(E5M2X4),
+                        rhs_scale=g_scales[:, i, sl // 4, :],
+                        start=first,
+                        stop=last,
+                    )
+
+        by_slice = result_pool.tile([P, SLICES, IMAGES], F32)
+        for sl in range(SLICES):
+            for ph in range(2):
+                rows = slice(ph * CHANNELS, (ph + 1) * CHANNELS)
+                wanted = acc[sl][rows, :].rearrange("q (n ph p2) -> q ph p2 n", ph=2, p2=4)[:, ph, sl % 4]
+                if sl % 2 == 0:
+                    nc.vector.tensor_copy(out=by_slice[rows, sl, :], in_=wanted)
+                else:
+                    nc.scalar.copy(out=by_slice[rows, sl, :], in_=wanted)
+        by_image = result_pool.tile([P, IMAGES, SLICES], F32)
+        half = IMAGES // 2
+        nc.vector.tensor_copy(
+            out=by_image[:, :half, :], in_=by_slice[:, :, :half].rearrange("q s n -> q n s")
+        )
+        nc.scalar.copy(out=by_image[:, half:, :], in_=by_slice[:, :, half:].rearrange("q s n -> q n s"))
+        nc.sync.dma_start(out=out_dram[0], in_=by_image[:CHANNELS, :, :])
+        nc.scalar.dma_start(out=out_dram[1], in_=by_image[CHANNELS:, :, :])

@@ -40,10 +40,10 @@ def tile_convdct_pa_k_kernel(tc, x_dct, k_dct, grad_out, out):
     )
     out_dram = out.rearrange("n c (ph yl) x -> ph c n (yl x)", ph=2)
 
-    with tc.tile_pool(name="g_raw", bufs=3) as g_raw_pool, tc.tile_pool(
-        name="k_raw", bufs=4
+    with tc.tile_pool(name="g_raw", bufs=4) as g_raw_pool, tc.tile_pool(
+        name="k_raw", bufs=5
     ) as k_raw_pool, tc.tile_pool(name="g_grp", bufs=2) as g_grp_pool, tc.tile_pool(
-        name="k_grp", bufs=2
+        name="k_grp", bufs=3
     ) as k_grp_pool, tc.tile_pool(name="g_mx", bufs=2) as g_mx_pool, tc.tile_pool(
         name="k_mx", bufs=3
     ) as k_mx_pool, tc.tile_pool(name="result", bufs=1) as result_pool, tc.psum_pool(
@@ -68,7 +68,7 @@ def tile_convdct_pa_k_kernel(tc, x_dct, k_dct, grad_out, out):
                         g_words = g_grp[:, i, mg, :].rearrange(
                             "q (n ph p2 j) -> q n ph j p2", n=IMAGE_CHUNK, ph=2, p2=4, j=PACK
                         )
-                        if mg == 0:
+                        if i == 0:
                             nc.vector.tensor_copy(out=g_words, in_=g_rows[:, i, mg])
                         else:
                             for ph in range(2):
@@ -96,11 +96,16 @@ def tile_convdct_pa_k_kernel(tc, x_dct, k_dct, grad_out, out):
                     "q (sc si ph c j) -> q ph sc c si j", sc=2, si=4, ph=2, c=CHANNELS, j=PACK
                 )
                 nc.vector.tensor_copy(out=k_words[:, 0], in_=k_rows[:, 0])
-                for sc in range(2):
-                    nc.scalar.copy(out=k_words[:, 1, sc], in_=k_rows[:, 1, sc])
+                nc.vector.tensor_copy(out=k_words[:, 1, 0], in_=k_rows[:, 1, 0])
+                nc.scalar.copy(out=k_words[:, 1, 1], in_=k_rows[:, 1, 1])
                 k_codes = k_mx_pool.tile([P, SLICES * M_STATIONARY], U32, align_bytes=64)
                 k_scales = k_mx_pool.tile([P, SLICES * M_STATIONARY], U8, align_bytes=64)
-                nc.vector.quantize_mx(out=k_codes[:].bitcast(E4M3X4), scales=k_scales[:], in_=k_grp[:])
+                for sc in range(2):
+                    words = slice(sc * 4 * M_STATIONARY, (sc + 1) * 4 * M_STATIONARY)
+                    values = slice(sc * 4 * M_STATIONARY * PACK, (sc + 1) * 4 * M_STATIONARY * PACK)
+                    nc.vector.quantize_mx(
+                        out=k_codes[:, words].bitcast(E4M3X4), scales=k_scales[:, words], in_=k_grp[:, values]
+                    )
 
                 first = cl == 0 and i == 0
                 last = cl == CLASSES - 1 and i == PASSES_PER_CLASS - 1
@@ -116,20 +121,17 @@ def tile_convdct_pa_k_kernel(tc, x_dct, k_dct, grad_out, out):
                         stop=last,
                     )
 
-        by_slice = result_pool.tile([P, SLICES, IMAGES], F32)
+        by_slice = result_pool.tile([P, SLICES, 2, IMAGES], F32)
         for sl in range(SLICES):
-            for ph in range(2):
-                rows = slice(ph * CHANNELS, (ph + 1) * CHANNELS)
-                wanted = acc[sl][rows, :].rearrange("q (n ph p2) -> q ph p2 n", ph=2, p2=4)[:, ph, sl % 4]
-                if sl % 2 == 0:
-                    nc.vector.tensor_copy(out=by_slice[rows, sl, :], in_=wanted)
-                else:
-                    nc.scalar.copy(out=by_slice[rows, sl, :], in_=wanted)
+            both = acc[sl][:].rearrange("q (n ph p2) -> q p2 ph n", ph=2, p2=4)[:, sl % 4]
+            if sl % 2 == 0:
+                nc.vector.tensor_copy(out=by_slice[:, sl], in_=both)
+            else:
+                nc.scalar.copy(out=by_slice[:, sl], in_=both)
         by_image = result_pool.tile([P, IMAGES, SLICES], F32)
-        half = IMAGES // 2
-        nc.vector.tensor_copy(
-            out=by_image[:, :half, :], in_=by_slice[:, :, :half].rearrange("q s n -> q n s")
-        )
-        nc.scalar.copy(out=by_image[:, half:, :], in_=by_slice[:, :, half:].rearrange("q s n -> q n s"))
-        nc.sync.dma_start(out=out_dram[0], in_=by_image[:CHANNELS, :, :])
-        nc.scalar.dma_start(out=out_dram[1], in_=by_image[CHANNELS:, :, :])
+        low = slice(0, CHANNELS)
+        high = slice(CHANNELS, 2 * CHANNELS)
+        nc.vector.tensor_copy(out=by_image[low], in_=by_slice[low, :, 0, :].rearrange("q s n -> q n s"))
+        nc.scalar.copy(out=by_image[high], in_=by_slice[high, :, 1, :].rearrange("q s n -> q n s"))
+        nc.sync.dma_start(out=out_dram[0], in_=by_image[low])
+        nc.scalar.dma_start(out=out_dram[1], in_=by_image[high])

@@ -45,81 +45,89 @@ def tile_convdct_pa_k_kernel(tc, x_dct, k_dct, grad_out, out):
     ) as k_raw_pool, tc.tile_pool(name="g_grp", bufs=2) as g_grp_pool, tc.tile_pool(
         name="k_grp", bufs=3
     ) as k_grp_pool, tc.tile_pool(name="g_mx", bufs=2) as g_mx_pool, tc.tile_pool(
-        name="k_mx", bufs=3
+        name="k_mx", bufs=4
     ) as k_mx_pool, tc.tile_pool(name="result", bufs=1) as result_pool, tc.psum_pool(
         name="acc", bufs=1
     ) as acc_pool:
         acc = [acc_pool.tile([P, N_MOVING], F32, name="acc%d" % sl) for sl in range(SLICES)]
 
+        def quantise_g_chunk(cl, chunk, g_codes, g_scales):
+            images = slice(chunk * IMAGE_CHUNK, (chunk + 1) * IMAGE_CHUNK)
+            g_raw = g_raw_pool.tile([P, IMAGE_CHUNK, RUN * FREQS], BF16)
+            for hf in range(HALVES):
+                nc.sync.dma_start(out=g_raw[hf:P:2, :, :], in_=g_dram[cl, hf, :, images, :])
+            g_rows = g_raw[:].rearrange(
+                "q n (i j ph mg p2) -> q i mg n ph j p2", i=PASSES_PER_CLASS, j=PACK, ph=2, mg=2, p2=4
+            )
+            g_grp = g_grp_pool.tile([P, PASSES_PER_CLASS, 2, IMAGE_CHUNK * 8 * PACK], BF16, align_bytes=64)
+            for i in range(PASSES_PER_CLASS):
+                for mg in range(2):
+                    g_words = g_grp[:, i, mg, :].rearrange(
+                        "q (n ph p2 j) -> q n ph j p2", n=IMAGE_CHUNK, ph=2, p2=4, j=PACK
+                    )
+                    if mg == 0:
+                        nc.vector.tensor_copy(out=g_words, in_=g_rows[:, i, mg])
+                    else:
+                        for ph in range(2):
+                            nc.scalar.copy(out=g_words[:, :, ph], in_=g_rows[:, i, mg, :, ph])
+            columns = slice(chunk * IMAGE_CHUNK * 8, (chunk + 1) * IMAGE_CHUNK * 8)
+            for i in range(PASSES_PER_CLASS):
+                for mg in range(2):
+                    nc.vector.quantize_mx(
+                        out=g_codes[:, i, mg, columns].bitcast(E5M2X4),
+                        scales=g_scales[:, i, mg, columns],
+                        in_=g_grp[:, i, mg, :],
+                    )
+
+        def quantise_k_pass(cl, i):
+            k_raw = k_raw_pool.tile([P, PACK, CHANNELS * FREQS], BF16)
+            for hf in range(HALVES):
+                nc.sync.dma_start(
+                    out=k_raw[hf:P:2, :, :], in_=k_dram[cl, hf, :, i * PACK : (i + 1) * PACK, :]
+                )
+            k_rows = k_raw[:].rearrange("q j (c ph sc si) -> q ph sc c si j", c=CHANNELS, ph=2, sc=2, si=4)
+            k_grp = k_grp_pool.tile([P, SLICES * M_STATIONARY * PACK], BF16, align_bytes=64)
+            k_words = k_grp[:].rearrange(
+                "q (sc si ph c j) -> q ph sc c si j", sc=2, si=4, ph=2, c=CHANNELS, j=PACK
+            )
+            nc.vector.tensor_copy(out=k_words[:, 0], in_=k_rows[:, 0])
+            for sc in range(2):
+                nc.scalar.copy(out=k_words[:, 1, sc], in_=k_rows[:, 1, sc])
+            k_codes = k_mx_pool.tile([P, SLICES * M_STATIONARY], U32, align_bytes=64)
+            k_scales = k_mx_pool.tile([P, SLICES * M_STATIONARY], U8, align_bytes=64)
+            for sc in range(2):
+                words = slice(sc * 4 * M_STATIONARY, (sc + 1) * 4 * M_STATIONARY)
+                values = slice(sc * 4 * M_STATIONARY * PACK, (sc + 1) * 4 * M_STATIONARY * PACK)
+                nc.vector.quantize_mx(
+                    out=k_codes[:, words].bitcast(E4M3X4), scales=k_scales[:, words], in_=k_grp[:, values]
+                )
+            return k_codes, k_scales
+
+        def multiply(cl, i, k_mx, g_codes, g_scales):
+            k_codes, k_scales = k_mx
+            for sl in range(SLICES):
+                m_cols = slice(sl * M_STATIONARY, (sl + 1) * M_STATIONARY)
+                nc.tensor.matmul_mx(
+                    out=acc[sl][:],
+                    lhsT=k_codes[:, m_cols].bitcast(E4M3X4),
+                    lhsT_scale=k_scales[:, m_cols],
+                    rhs=g_codes[:, i, sl // 4, :].bitcast(E5M2X4),
+                    rhs_scale=g_scales[:, i, sl // 4, :],
+                    start=(cl == 0 and i == 0),
+                    stop=(cl == CLASSES - 1 and i == PASSES_PER_CLASS - 1),
+                )
+
         for cl in range(CLASSES):
             g_codes = g_mx_pool.tile([P, PASSES_PER_CLASS, 2, N_MOVING], U32, align_bytes=64)
             g_scales = g_mx_pool.tile([P, PASSES_PER_CLASS, 2, N_MOVING], U8, align_bytes=64)
+            early = []
             for chunk in range(CHUNKS):
-                images = slice(chunk * IMAGE_CHUNK, (chunk + 1) * IMAGE_CHUNK)
-                g_raw = g_raw_pool.tile([P, IMAGE_CHUNK, RUN * FREQS], BF16)
-                for hf in range(HALVES):
-                    nc.sync.dma_start(out=g_raw[hf:P:2, :, :], in_=g_dram[cl, hf, :, images, :])
-                g_rows = g_raw[:].rearrange(
-                    "q n (i j ph mg p2) -> q i mg n ph j p2", i=PASSES_PER_CLASS, j=PACK, ph=2, mg=2, p2=4
-                )
-                g_grp = g_grp_pool.tile([P, PASSES_PER_CLASS, 2, IMAGE_CHUNK * 8 * PACK], BF16, align_bytes=64)
-                for i in range(PASSES_PER_CLASS):
-                    for mg in range(2):
-                        g_words = g_grp[:, i, mg, :].rearrange(
-                            "q (n ph p2 j) -> q n ph j p2", n=IMAGE_CHUNK, ph=2, p2=4, j=PACK
-                        )
-                        if i == 0:
-                            nc.vector.tensor_copy(out=g_words, in_=g_rows[:, i, mg])
-                        else:
-                            for ph in range(2):
-                                nc.scalar.copy(out=g_words[:, :, ph], in_=g_rows[:, i, mg, :, ph])
-                columns = slice(chunk * IMAGE_CHUNK * 8, (chunk + 1) * IMAGE_CHUNK * 8)
-                for i in range(PASSES_PER_CLASS):
-                    for mg in range(2):
-                        nc.vector.quantize_mx(
-                            out=g_codes[:, i, mg, columns].bitcast(E5M2X4),
-                            scales=g_scales[:, i, mg, columns],
-                            in_=g_grp[:, i, mg, :],
-                        )
-
-            for i in range(PASSES_PER_CLASS):
-                k_raw = k_raw_pool.tile([P, PACK, CHANNELS * FREQS], BF16)
-                for hf in range(HALVES):
-                    nc.sync.dma_start(
-                        out=k_raw[hf:P:2, :, :], in_=k_dram[cl, hf, :, i * PACK : (i + 1) * PACK, :]
-                    )
-                k_rows = k_raw[:].rearrange(
-                    "q j (c ph sc si) -> q ph sc c si j", c=CHANNELS, ph=2, sc=2, si=4
-                )
-                k_grp = k_grp_pool.tile([P, SLICES * M_STATIONARY * PACK], BF16, align_bytes=64)
-                k_words = k_grp[:].rearrange(
-                    "q (sc si ph c j) -> q ph sc c si j", sc=2, si=4, ph=2, c=CHANNELS, j=PACK
-                )
-                nc.vector.tensor_copy(out=k_words[:, 0], in_=k_rows[:, 0])
-                nc.vector.tensor_copy(out=k_words[:, 1, 0], in_=k_rows[:, 1, 0])
-                nc.scalar.copy(out=k_words[:, 1, 1], in_=k_rows[:, 1, 1])
-                k_codes = k_mx_pool.tile([P, SLICES * M_STATIONARY], U32, align_bytes=64)
-                k_scales = k_mx_pool.tile([P, SLICES * M_STATIONARY], U8, align_bytes=64)
-                for sc in range(2):
-                    words = slice(sc * 4 * M_STATIONARY, (sc + 1) * 4 * M_STATIONARY)
-                    values = slice(sc * 4 * M_STATIONARY * PACK, (sc + 1) * 4 * M_STATIONARY * PACK)
-                    nc.vector.quantize_mx(
-                        out=k_codes[:, words].bitcast(E4M3X4), scales=k_scales[:, words], in_=k_grp[:, values]
-                    )
-
-                first = cl == 0 and i == 0
-                last = cl == CLASSES - 1 and i == PASSES_PER_CLASS - 1
-                for sl in range(SLICES):
-                    m_cols = slice(sl * M_STATIONARY, (sl + 1) * M_STATIONARY)
-                    nc.tensor.matmul_mx(
-                        out=acc[sl][:],
-                        lhsT=k_codes[:, m_cols].bitcast(E4M3X4),
-                        lhsT_scale=k_scales[:, m_cols],
-                        rhs=g_codes[:, i, sl // 4, :].bitcast(E5M2X4),
-                        rhs_scale=g_scales[:, i, sl // 4, :],
-                        start=first,
-                        stop=last,
-                    )
+                early.append(quantise_k_pass(cl, chunk))
+                quantise_g_chunk(cl, chunk, g_codes, g_scales)
+            for i in range(CHUNKS):
+                multiply(cl, i, early[i], g_codes, g_scales)
+            for i in range(CHUNKS, PASSES_PER_CLASS):
+                multiply(cl, i, quantise_k_pass(cl, i), g_codes, g_scales)
 
         by_slice = result_pool.tile([P, SLICES, 2, IMAGES], F32)
         for sl in range(SLICES):

@@ -36,7 +36,7 @@ def tile_convdct_pa_k_kernel(tc, x_dct, k_dct, grad_out, out):
         "n (m cl hf e) y x -> cl hf m n (e y x)", m=64, cl=CLASSES, hf=HALVES, e=RUN
     )
     k_dram = k_dct.rearrange(
-        "(m cl hf e) c y x -> cl hf m e (c y x)", m=64, cl=CLASSES, hf=HALVES, e=RUN
+        "(m cl hf e) c y x -> cl m hf (e c y x)", m=64, cl=CLASSES, hf=HALVES, e=RUN
     )
     out_dram = out.rearrange("n c (ph yl) x -> ph c n (yl x)", ph=2)
 
@@ -81,10 +81,10 @@ def tile_convdct_pa_k_kernel(tc, x_dct, k_dct, grad_out, out):
 
         def quantise_k_pass(cl, i):
             k_raw = k_raw_pool.tile([P, PACK, CHANNELS * FREQS], BF16)
-            for hf in range(HALVES):
-                nc.sync.dma_start(
-                    out=k_raw[hf:P:2, :, :], in_=k_dram[cl, hf, :, i * PACK : (i + 1) * PACK, :]
-                )
+            row = PACK * CHANNELS * FREQS
+            nc.sync.dma_start(
+                out=k_raw[:].rearrange("q j z -> q (j z)"), in_=k_dram[cl, :, :, i * row : (i + 1) * row]
+            )
             k_rows = k_raw[:].rearrange("q j (c ph sc si) -> q ph sc c si j", c=CHANNELS, ph=2, sc=2, si=4)
             k_grp = k_grp_pool.tile([P, SLICES * M_STATIONARY * PACK], BF16, align_bytes=64)
             k_words = k_grp[:].rearrange(

@@ -21,7 +21,9 @@ RUN = PASSES_PER_CLASS * PACK
 
 SLICES = 8
 IMAGE_CHUNK = 32
-CHUNKS = IMAGES // IMAGE_CHUNK
+CHUNKS = ((0, 32), (32, 32))
+HEAD_CHUNKS = ((0, 16), (16, 16), (32, 32))
+EARLY_PASSES = 2
 N_MOVING = 512
 M_STATIONARY = 128
 
@@ -51,26 +53,26 @@ def tile_convdct_pa_k_kernel(tc, x_dct, k_dct, grad_out, out):
     ) as acc_pool:
         acc = [acc_pool.tile([P, N_MOVING], F32, name="acc%d" % sl) for sl in range(SLICES)]
 
-        def quantise_g_chunk(cl, chunk, g_codes, g_scales):
-            images = slice(chunk * IMAGE_CHUNK, (chunk + 1) * IMAGE_CHUNK)
-            g_raw = g_raw_pool.tile([P, IMAGE_CHUNK, RUN * FREQS], BF16)
+        def quantise_g_chunk(cl, first, count, g_codes, g_scales):
+            images = slice(first, first + count)
+            g_raw = g_raw_pool.tile([P, count, RUN * FREQS], BF16)
             for hf in range(HALVES):
                 nc.sync.dma_start(out=g_raw[hf:P:2, :, :], in_=g_dram[cl, hf, :, images, :])
             g_rows = g_raw[:].rearrange(
                 "q n (i j ph mg p2) -> q i mg n ph j p2", i=PASSES_PER_CLASS, j=PACK, ph=2, mg=2, p2=4
             )
-            g_grp = g_grp_pool.tile([P, PASSES_PER_CLASS, 2, IMAGE_CHUNK * 8 * PACK], BF16, align_bytes=64)
+            g_grp = g_grp_pool.tile([P, PASSES_PER_CLASS, 2, count * 8 * PACK], BF16, align_bytes=64)
             for i in range(PASSES_PER_CLASS):
                 for mg in range(2):
                     g_words = g_grp[:, i, mg, :].rearrange(
-                        "q (n ph p2 j) -> q n ph j p2", n=IMAGE_CHUNK, ph=2, p2=4, j=PACK
+                        "q (n ph p2 j) -> q n ph j p2", n=count, ph=2, p2=4, j=PACK
                     )
                     if mg == 0:
                         nc.vector.tensor_copy(out=g_words, in_=g_rows[:, i, mg])
                     else:
                         for ph in range(2):
                             nc.scalar.copy(out=g_words[:, :, ph], in_=g_rows[:, i, mg, :, ph])
-            columns = slice(chunk * IMAGE_CHUNK * 8, (chunk + 1) * IMAGE_CHUNK * 8)
+            columns = slice(first * 8, (first + count) * 8)
             for i in range(PASSES_PER_CLASS):
                 for mg in range(2):
                     nc.vector.quantize_mx(
@@ -120,13 +122,15 @@ def tile_convdct_pa_k_kernel(tc, x_dct, k_dct, grad_out, out):
         for cl in range(CLASSES):
             g_codes = g_mx_pool.tile([P, PASSES_PER_CLASS, 2, N_MOVING], U32, align_bytes=64)
             g_scales = g_mx_pool.tile([P, PASSES_PER_CLASS, 2, N_MOVING], U8, align_bytes=64)
+            early_passes = 0 if cl == CLASSES - 1 else EARLY_PASSES
             early = []
-            for chunk in range(CHUNKS):
-                early.append(quantise_k_pass(cl, chunk))
-                quantise_g_chunk(cl, chunk, g_codes, g_scales)
-            for i in range(CHUNKS):
+            for first, count in HEAD_CHUNKS if cl == 0 else CHUNKS:
+                if first % IMAGE_CHUNK == 0 and len(early) < early_passes:
+                    early.append(quantise_k_pass(cl, len(early)))
+                quantise_g_chunk(cl, first, count, g_codes, g_scales)
+            for i in range(early_passes):
                 multiply(cl, i, early[i], g_codes, g_scales)
-            for i in range(CHUNKS, PASSES_PER_CLASS):
+            for i in range(early_passes, PASSES_PER_CLASS):
                 multiply(cl, i, quantise_k_pass(cl, i), g_codes, g_scales)
 
         by_slice = result_pool.tile([P, SLICES, 2, IMAGES], F32)

import concourse.mybir as mybir

BF16 = mybir.dt.bfloat16
F32 = mybir.dt.float32
U32 = mybir.dt.uint32
U8 = mybir.dt.uint8
E4M3X4 = mybir.dt.float8_e4m3fn_x4
E5M2X4 = mybir.dt.float8_e5m2_x4

P = 128
IMAGES = 64
CHANNELS = 64
FILTERS = 8192
FREQS = 16

CLASSES = 4
HALVES = 2
PASSES_PER_CLASS = 4
PACK = 4
RUN = PASSES_PER_CLASS * PACK

SLICES = 8
IMAGE_CHUNK = 32
CHUNKS = ((0, 32), (32, 32))
HEAD_CHUNKS = ((0, 16), (16, 16), (32, 32))
EARLY_PASSES = 2
N_MOVING = 512
M_STATIONARY = 128

FLOPS = 2 * FREQS * IMAGES * CHANNELS * FILTERS
BYTES = 2 * FILTERS * FREQS * (IMAGES + CHANNELS) + 4 * IMAGES * CHANNELS * FREQS


def tile_convdct_pa_k_kernel(tc, x_dct, k_dct, grad_out, out):
    nc = tc.nc

    g_dram = grad_out.rearrange(
        "n (m cl hf e) y x -> cl hf m n (e y x)", m=64, cl=CLASSES, hf=HALVES, e=RUN
    )
    k_dram = k_dct.rearrange(
        "(m cl hf e) c y x -> cl m hf (e c y x)", m=64, cl=CLASSES, hf=HALVES, e=RUN
    )
    out_dram = out.rearrange("n c (ph yl) x -> ph c n (yl x)", ph=2)

    with tc.tile_pool(name="g_raw", bufs=4) as g_raw_pool, tc.tile_pool(
        name="k_raw", bufs=5
    ) as k_raw_pool, tc.tile_pool(name="g_grp", bufs=2) as g_grp_pool, tc.tile_pool(
        name="k_grp", bufs=3
    ) as k_grp_pool, tc.tile_pool(name="g_mx", bufs=2) as g_mx_pool, tc.tile_pool(
        name="k_mx", bufs=4
    ) as k_mx_pool, tc.tile_pool(name="result", bufs=1) as result_pool, tc.psum_pool(
        name="acc", bufs=1
    ) as acc_pool:
        acc = [acc_pool.tile([P, N_MOVING], F32, name="acc%d" % sl) for sl in range(SLICES)]

        def quantise_g_chunk(cl, first, count, g_codes, g_scales):
            images = slice(first, first + count)
            g_raw = g_raw_pool.tile([P, count, RUN * FREQS], BF16)
            for hf in range(HALVES):
                nc.sync.dma_start(out=g_raw[hf:P:2, :, :], in_=g_dram[cl, hf, :, images, :])
            g_rows = g_raw[:].rearrange(
                "q n (i j ph mg p2) -> q i mg n ph j p2", i=PASSES_PER_CLASS, j=PACK, ph=2, mg=2, p2=4
            )
            g_grp = g_grp_pool.tile([P, PASSES_PER_CLASS, 2, count * 8 * PACK], BF16, align_bytes=64)
            for i in range(PASSES_PER_CLASS):
                for mg in range(2):
                    g_words = g_grp[:, i, mg, :].rearrange(
                        "q (n ph p2 j) -> q n ph j p2", n=count, ph=2, p2=4, j=PACK
                    )
                    if mg == 0:
                        nc.vector.tensor_copy(out=g_words, in_=g_rows[:, i, mg])
                    else:
                        for ph in range(2):
                            nc.scalar.copy(out=g_words[:, :, ph], in_=g_rows[:, i, mg, :, ph])
            columns = slice(first * 8, (first + count) * 8)
            for i in range(PASSES_PER_CLASS):
                for mg in range(2):
                    nc.vector.quantize_mx(
                        out=g_codes[:, i, mg, columns].bitcast(E5M2X4),
                        scales=g_scales[:, i, mg, columns],
                        in_=g_grp[:, i, mg, :],
                    )

        def quantise_k_pass(cl, i):
            k_raw = k_raw_pool.tile([P, PACK, CHANNELS * FREQS], BF16)
            row = PACK * CHANNELS * FREQS
            nc.sync.dma_start(
                out=k_raw[:].rearrange("q j z -> q (j z)"), in_=k_dram[cl, :, :, i * row : (i + 1) * row]
            )
            k_rows = k_raw[:].rearrange("q j (c ph sc si) -> q ph sc c si j", c=CHANNELS, ph=2, sc=2, si=4)
            k_grp = k_grp_pool.tile([P, SLICES * M_STATIONARY * PACK], BF16, align_bytes=64)
            k_words = k_grp[:].rearrange(
                "q (sc si ph c j) -> q ph sc c si j", sc=2, si=4, ph=2, c=CHANNELS, j=PACK
            )
            nc.vector.tensor_copy(out=k_words[:, 0], in_=k_rows[:, 0])
            for sc in range(2):
                nc.scalar.copy(out=k_words[:, 1, sc], in_=k_rows[:, 1, sc])
            k_codes = k_mx_pool.tile([P, SLICES * M_STATIONARY], U32, align_bytes=64)
            k_scales = k_mx_pool.tile([P, SLICES * M_STATIONARY], U8, align_bytes=64)
            for sc in range(2):
                words = slice(sc * 4 * M_STATIONARY, (sc + 1) * 4 * M_STATIONARY)
                values = slice(sc * 4 * M_STATIONARY * PACK, (sc + 1) * 4 * M_STATIONARY * PACK)
                nc.vector.quantize_mx(
                    out=k_codes[:, words].bitcast(E4M3X4), scales=k_scales[:, words], in_=k_grp[:, values]
                )
            return k_codes, k_scales

        def multiply(cl, i, k_mx, g_codes, g_scales):
            k_codes, k_scales = k_mx
            for sl in range(SLICES):
                m_cols = slice(sl * M_STATIONARY, (sl + 1) * M_STATIONARY)
                nc.tensor.matmul_mx(
                    out=acc[sl][:],
                    lhsT=k_codes[:, m_cols].bitcast(E4M3X4),
                    lhsT_scale=k_scales[:, m_cols],
                    rhs=g_codes[:, i, sl // 4, :].bitcast(E5M2X4),
                    rhs_scale=g_scales[:, i, sl // 4, :],
                    start=(cl == 0 and i == 0),
                    stop=(cl == CLASSES - 1 and i == PASSES_PER_CLASS - 1),
                )

        for cl in range(CLASSES):
            g_codes = g_mx_pool.tile([P, PASSES_PER_CLASS, 2, N_MOVING], U32, align_bytes=64)
            g_scales = g_mx_pool.tile([P, PASSES_PER_CLASS, 2, N_MOVING], U8, align_bytes=64)
            early_passes = 0 if cl == CLASSES - 1 else EARLY_PASSES
            early = []
            for first, count in HEAD_CHUNKS if cl == 0 else CHUNKS:
                if first % IMAGE_CHUNK == 0 and len(early) < early_passes:
                    early.append(quantise_k_pass(cl, len(early)))
                quantise_g_chunk(cl, first, count, g_codes, g_scales)
            for i in range(early_passes):
                multiply(cl, i, early[i], g_codes, g_scales)
            for i in range(early_passes, PASSES_PER_CLASS):
                multiply(cl, i, quantise_k_pass(cl, i), g_codes, g_scales)

        by_slice = result_pool.tile([P, SLICES, 2, IMAGES], F32)
        for sl in range(SLICES):
            both = acc[sl][:].rearrange("q (n ph p2) -> q p2 ph n", ph=2, p2=4)[:, sl % 4]
            if sl % 2 == 0:
                nc.vector.tensor_copy(out=by_slice[:, sl], in_=both)
            else:
                nc.scalar.copy(out=by_slice[:, sl], in_=both)
        by_image = result_pool.tile([P, IMAGES, SLICES], F32)
        low = slice(0, CHANNELS)
        high = slice(CHANNELS, 2 * CHANNELS)
        nc.vector.tensor_copy(out=by_image[low], in_=by_slice[low, :, 0, :].rearrange("q s n -> q n s"))
        nc.scalar.copy(out=by_image[high], in_=by_slice[high, :, 1, :].rearrange("q s n -> q n s"))
        nc.sync.dma_start(out=out_dram[0], in_=by_image[low])
        nc.scalar.dma_start(out=out_dram[1], in_=by_image[high])
